import numpy as np
import ml_dtypes


def mxq(x, axis, fmt="e4m3"):
    dtype, down = {"e4m3": (ml_dtypes.float8_e4m3fn, 7), "e5m2": (ml_dtypes.float8_e5m2, 14)}[fmt]
    v = np.moveaxis(np.asarray(x, np.float32).astype(ml_dtypes.bfloat16).astype(np.float64), axis, -1)
    blocks = v.reshape(v.shape[:-1] + (-1, 32))
    amax = np.abs(blocks).max(-1, keepdims=True)
    byte = np.maximum(np.where(amax > 0, np.frexp(amax)[1] - 1 + 127, 0) - down, 1)
    scale = np.exp2(byte - 127.0)
    codes = (blocks / scale).astype(np.float32).astype(dtype).astype(np.float64)
    return np.moveaxis((codes * scale).reshape(v.shape), -1, axis)


WIDE = False


def mx_kscale(k):
    if not WIDE:
        return np.ones(k)
    levels = np.array([10, -10, 5, -5, 0])
    a = np.random.permutation(np.resize(levels, k // 512 * 4)).reshape(k // 512, 4)
    idx = np.arange(k)
    return np.exp2(a[idx // 512, idx % 128 // 32])


BF16 = ml_dtypes.bfloat16


def bf(x):
    return np.asarray(x, np.float32).astype(BF16)


def f64(x):
    return np.asarray(x).astype(np.float64)


E2M1 = np.array([0.0, 0.5, 1.0, 1.5, 2.0, 3.0, 4.0, 6.0, -0.0, -0.5, -1.0, -1.5, -2.0, -3.0, -4.0, -6.0])


def pack_weight(w, fmt):
    k, n = w.shape
    w = f64(bf(w)).reshape(k // 32, 32, n)
    amax = np.abs(w).max(1)
    if fmt == "e4m3":
        byte = np.frexp(amax)[1] - 1 + 127 - 7
    else:
        mant, ex = np.frexp(amax / 6.0)
        byte = np.where(mant > 0.5, ex, ex - 1) + 127
    byte = np.clip(np.where(amax > 0, byte, 1), 1, 254)
    scaled = (w * np.exp2(127.0 - byte)[:, None, :]).reshape(k, n).astype(np.float32)
    by_word = np.ascontiguousarray(scaled.reshape(k // 512, 128, 4, n).transpose(0, 1, 3, 2))
    if fmt == "e4m3":
        words = by_word.astype(ml_dtypes.float8_e4m3fn).view(np.uint8)
    else:
        c = by_word.astype(ml_dtypes.float4_e2m1fn).view(np.uint8) & 0xF
        words = c[..., 0::2] | (c[..., 1::2] << 4)
    return np.ascontiguousarray(words), np.ascontiguousarray(byte.astype(np.uint8).reshape(k // 512, 16, n))


def unpack_weight(words, scales, fmt):
    g, p, n, _ = words.shape
    if fmt == "e4m3":
        vals = np.ascontiguousarray(words).view(ml_dtypes.float8_e4m3fn).astype(np.float64)
    else:
        nib = np.empty((g, p, n, 4), np.uint8)
        nib[..., 0::2] = words & 0xF
        nib[..., 1::2] = words >> 4
        vals = E2M1[nib]
    vals = vals * np.repeat(np.exp2(scales.astype(np.float64) - 127.0), 8, axis=1)[..., None]
    return vals.transpose(0, 1, 3, 2).reshape(g * 512, n)


N, NR, F, C, R = 512, 1024, 8192, 128, 8
EPS = 1e-8
FMT = "e4m3"


def encode_amplitude(v):
    return v / (np.linalg.norm(v, axis=1, keepdims=True) + EPS)


def setup_inputs():
    s = mx_kscale(F)
    basis = np.random.standard_normal((R, F)) / np.sqrt(R)
    x = np.random.standard_normal((N, R)) @ basis + 0.5 * np.random.standard_normal((N, F))
    x_ref = np.random.standard_normal((NR, R)) @ basis + 0.5 * np.random.standard_normal((NR, F))
    c = 2.0 ** np.round(np.log2(np.mean(s ** 2) * np.mean(s ** -2.0)))
    mean_ = bf(np.random.standard_normal(F) * 0.5 * np.minimum(s, 1.0 / s))
    components_ = np.random.standard_normal((C, NR)) * 8.0 / np.sqrt(NR) * c
    words, scales = pack_weight(components_.T, FMT)
    return {"x": bf(x * s), "x_ref": bf(x_ref / s),
            "mean_": mean_,
            "components__words": words, "components__scales": scales}


def reference(x, x_ref, mean_, components__words, components__scales):
    xs = f64(x) - f64(mean_)
    xr = f64(x_ref) - f64(mean_)
    s1 = encode_amplitude(xs)
    s2 = encode_amplitude(xr)
    ov = mxq(s1, 1, "e4m3") @ mxq(s2, 1, "e4m3").T
    K = ov * ov
    return mxq(K, 1, "e4m3") @ unpack_weight(components__words, components__scales, FMT)

@@ -1,0 +1,296 @@
+from contextlib import ExitStack
+
+import concourse.mybir as mybir
+from concourse.masks import make_identity
+
+BF16 = mybir.dt.bfloat16
+F32 = mybir.dt.float32
+I32 = mybir.dt.int32
+U32 = mybir.dt.uint32
+U8 = mybir.dt.uint8
+FP8X4 = mybir.dt.float8_e4m3fn_x4
+ALU = mybir.AluOpType
+ACT = mybir.ActivationFunctionType
+AXIS = mybir.AxisListType
+
+N_X = 512
+N_REF = 1024
+FEATURES = 8192
+COMPONENTS = 128
+EPS = 1e-8
+
+P = 128
+PACK = 4
+K_PASS = P * PACK
+PASSES = FEATURES // K_PASS
+REF_PASSES = N_REF // K_PASS
+SLAB_ROWS = P // PACK
+SLAB_COLS = FEATURES // PACK
+SLABS = P // SLAB_ROWS
+BANK_BF16 = 1024
+PASSES_PER_BANK = BANK_BF16 // K_PASS
+GROUPS = (N_X + N_REF) // P
+X_GROUPS = N_X // P
+QUARTERS = GROUPS * SLABS
+QUARTER_PASSES = PASSES // SLABS
+QUARTER_BANKS = QUARTER_PASSES // PASSES_PER_BANK
+
+LOAD_LAG = -6
+SUBTRACT_LAG = 0
+SQUARE_LAG = SUBTRACT_LAG + 1
+NORM_LAG = SQUARE_LAG + 1
+SCALE_LAG = NORM_LAG + (SLABS - 1)
+TURN_LAG = SCALE_LAG + (SLABS - 1) + 1
+QUANTISE_LAG = TURN_LAG + 1
+OVERLAP_LAG = QUANTISE_LAG + 1
+FIDELITY_LAG = OVERLAP_LAG + 1
+FIDELITY_QUANTISE_LAG = FIDELITY_LAG + 1
+
+FLOPS = 2 * N_X * N_REF * FEATURES + 2 * N_X * N_REF * COMPONENTS
+
+
+def tile_quantumkernelpca_kernel(tc, x, x_ref, mean_, components__words, components__scales, out):
+    nc = tc.nc
+    with ExitStack() as ctx:
+        const = ctx.enter_context(tc.tile_pool(name="const", bufs=1))
+        raw_pool = ctx.enter_context(tc.tile_pool(name="raw", bufs=8))
+        diff_pool = ctx.enter_context(tc.tile_pool(name="diff", bufs=8))
+        unit_pool = ctx.enter_context(tc.tile_pool(name="unit", bufs=8))
+        scratch = ctx.enter_context(tc.tile_pool(name="scratch", bufs=1))
+        stats = ctx.enter_context(tc.tile_pool(name="stats", bufs=3))
+        grouped_pool = ctx.enter_context(tc.tile_pool(name="grouped", bufs=4))
+        ref_pool = ctx.enter_context(tc.tile_pool(name="ref", bufs=2))
+        fid_pool = ctx.enter_context(tc.tile_pool(name="fid", bufs=2))
+        psum_mean = ctx.enter_context(tc.psum_pool(name="psum_mean", bufs=1))
+        psum_turn = ctx.enter_context(tc.psum_pool(name="psum_turn", bufs=3))
+        psum_ov = ctx.enter_context(tc.psum_pool(name="psum_ov", bufs=2))
+        psum_small = ctx.enter_context(tc.psum_pool(name="psum_small", bufs=1))
+        ctx.enter_context(tc.manual_schedule())
+
+        ident = const.tile([P, P], BF16)
+        make_identity(nc, ident[:])
+        warm = const.tile([P, 1], F32)
+        nc.vector.memset(warm[:], 1.0)
+        nc.scalar.activation(out=warm[:], in_=warm[:], func=ACT.Sqrt)
+        pick = const.tile([P, SLAB_ROWS, PACK], BF16)
+        nc.vector.tensor_copy(out=pick[:], in_=ident[:, 0:PACK].unsqueeze(1).to_broadcast([P, SLAB_ROWS, PACK]))
+        row_of = const.tile([P, SLAB_ROWS], F32)
+        nc.vector.tensor_reduce(
+            out=row_of[:], in_=ident[:].rearrange("p (r t) -> p r t", t=PACK), axis=AXIS.X, op=ALU.add
+        )
+        same_row = const.tile([P, SLAB_ROWS, PACK], F32)
+        nc.vector.tensor_copy(out=same_row[:], in_=row_of[:].unsqueeze(2).to_broadcast([P, SLAB_ROWS, PACK]))
+
+        mean_rows = const.tile([P, SLAB_COLS], BF16)
+        nc.vector.memset(mean_rows[:].bitcast(I32), 0)
+        nc.sync.dma_start(
+            out=mean_rows[0:PACK, :].rearrange("t (g j) -> t g j", j=P),
+            in_=mean_.rearrange("(g t j) -> t g j", t=PACK, j=P),
+        )
+        mean_lo = psum_mean.tile([P, BANK_BF16], BF16)
+        mean_hi = psum_mean.tile([P, BANK_BF16], BF16)
+        mean_banks = [mean_lo, mean_hi]
+        for h in range(2):
+            for c in range(2):
+                nc.tensor.matmul(
+                    out=mean_banks[h][:, 512 * c : 512 * (c + 1)],
+                    lhsT=pick[:].rearrange("p r t -> p (r t)"),
+                    rhs=mean_rows[:, BANK_BF16 * h + 512 * c : BANK_BF16 * h + 512 * (c + 1)],
+                    start=True,
+                    stop=True,
+                )
+
+        w_words = const.tile([P, REF_PASSES, COMPONENTS], U32, align_bytes=64)
+        w_scales = const.tile([P, REF_PASSES, COMPONENTS], U8, align_bytes=64)
+        nc.vector.memset(w_scales[:].rearrange("p h n -> p (h n)").bitcast(I32), 0)
+        x_codes = const.tile([P, PASSES, N_X], U32, align_bytes=64)
+        x_scales = const.tile([P, PASSES, N_X], U8, align_bytes=64)
+        fid_codes = const.tile([P, REF_PASSES, N_X], U32, align_bytes=64)
+        fid_scales = const.tile([P, REF_PASSES, N_X], U8, align_bytes=64)
+
+        x_groups = x.rearrange("(c q) (g t j) -> c t q g j", q=P, t=PACK, j=P)
+        ref_groups = x_ref.rearrange("(h q u) (g t j) -> h u t q g j", q=P, u=PACK, t=PACK, j=P)
+        rows_of = [x_groups[c] for c in range(X_GROUPS)]
+        rows_of += [ref_groups[h, u] for h in range(REF_PASSES) for u in range(PACK)]
+
+        raws, diffs, units, sumsqs, invs, turneds, groupeds = {}, {}, {}, {}, {}, {}, {}
+        codes_of, scales_of, overlaps, fids = {}, {}, {}, {}
+
+        def load(k):
+            n, a = divmod(k, SLABS)
+            raw = raw_pool.tile([P, SLAB_COLS], BF16)
+            for t in range(PACK):
+                nc.sync.dma_start(
+                    out=raw[t:P:PACK, :].rearrange("r (g j) -> r g j", j=P),
+                    in_=rows_of[n][t, SLAB_ROWS * a : SLAB_ROWS * (a + 1)],
+                )
+            raws[k] = raw
+
+        def subtract_mean(k):
+            diff = diff_pool.tile([P, SLAB_COLS], F32)
+            for h in range(2):
+                cols = slice(BANK_BF16 * h, BANK_BF16 * (h + 1))
+                nc.vector.tensor_tensor(out=diff[:, cols], in0=raws[k][:, cols], in1=mean_banks[h][:], op=ALU.subtract)
+            diffs[k] = diff
+
+        def sum_squares(k):
+            n, a = divmod(k, SLABS)
+            if a == 0:
+                sumsq = stats.tile([P, SLABS], F32)
+                sumsqs[n] = sumsq
+            squares = scratch.tile([P, SLAB_COLS], BF16)
+            nc.scalar.activation(out=squares[:], in_=diffs[k][:], func=ACT.Square, accum_out=sumsqs[n][:, a : a + 1])
+
+        def invert_norms(n):
+            row_sumsq = psum_small.tile([P, SLABS], F32, tag="small")
+            nc.tensor.matmul(
+                out=row_sumsq[:], lhsT=same_row[:].rearrange("p r t -> p (r t)"), rhs=sumsqs[n][:], start=True, stop=True
+            )
+            norm = stats.tile([P, SLABS], F32)
+            nc.scalar.activation(out=norm[:], in_=row_sumsq[:], func=ACT.Sqrt)
+            inv = stats.tile([P, SLABS], F32)
+            nc.vector.tensor_scalar_add(out=inv[:], in0=norm[:], scalar1=EPS)
+            nc.vector.reciprocal(out=inv[:], in_=inv[:])
+            invs[n] = inv
+
+        def scale(k):
+            n, a = divmod(k, SLABS)
+            unit = unit_pool.tile([P, SLAB_COLS], BF16)
+            nc.gpsimd.tensor_scalar(
+                out=unit[:], in0=diffs[k][:], scalar1=invs[n][:, a : a + 1], scalar2=0.0, op0=ALU.mult, op1=ALU.add
+            )
+            units[k] = unit
+
+        def turn(k):
+            n, c = divmod(k, SLABS)
+            for b in range(QUARTER_BANKS):
+                turned = psum_turn.tile([P, PASSES_PER_BANK, SLABS, P], BF16)
+                for i in range(PASSES_PER_BANK):
+                    g = QUARTER_PASSES * c + PASSES_PER_BANK * b + i
+                    for a in range(SLABS):
+                        nc.tensor.transpose(turned[:, i, a, :], units[SLABS * n + a][:, P * g : P * (g + 1)], ident[:])
+                turneds[k, b] = turned
+
+        def copy_out(k):
+            for b in range(QUARTER_BANKS):
+                grouped = grouped_pool.tile([P, PASSES_PER_BANK, K_PASS], BF16, align_bytes=64)
+                flat_out = grouped[:].rearrange("p i c -> p (i c)")
+                flat_in = turneds[k, b][:].rearrange("p i a c -> p (i a c)")
+                if k % 2 == 1 and b == 1:
+                    nc.vector.tensor_copy(out=flat_out, in_=flat_in)
+                else:
+                    nc.scalar.copy(out=flat_out, in_=flat_in)
+                groupeds[k, b] = grouped
+
+        def quantise(k):
+            n, c = divmod(k, SLABS)
+            if c == 0:
+                if n < X_GROUPS:
+                    cols = slice(P * n, P * (n + 1))
+                    codes_of[n] = x_codes[:, :, cols]
+                    scales_of[n] = x_scales[:, :, cols]
+                else:
+                    ref_codes = ref_pool.tile([P, PASSES, P], U32, align_bytes=64)
+                    ref_scales = ref_pool.tile([P, PASSES, P], U8, align_bytes=64)
+                    codes_of[n] = ref_codes[:]
+                    scales_of[n] = ref_scales[:]
+            for b in range(QUARTER_BANKS):
+                for i in range(PASSES_PER_BANK):
+                    g = QUARTER_PASSES * c + PASSES_PER_BANK * b + i
+                    nc.vector.quantize_mx(
+                        out=codes_of[n][:, g, :].bitcast(FP8X4), scales=scales_of[n][:, g, :], in_=groupeds[k, b][:, i, :]
+                    )
+
+        def overlap_passes(k):
+            n, c = divmod(k, SLABS)
+            if n < X_GROUPS:
+                return
+            if c == 0:
+                overlap = psum_ov.tile([P, N_X], F32)
+                overlaps[n] = overlap
+            for g in range(QUARTER_PASSES * c, QUARTER_PASSES * (c + 1)):
+                nc.tensor.matmul_mx(
+                    out=overlaps[n][:],
+                    lhsT=codes_of[n][:, g, :].bitcast(FP8X4),
+                    lhsT_scale=scales_of[n][:, g, :],
+                    rhs=x_codes[:, g, :].bitcast(FP8X4),
+                    rhs_scale=x_scales[:, g, :],
+                    start=(g == 0),
+                    stop=(g == PASSES - 1),
+                )
+
+        def square_overlap(n):
+            h, u = divmod(n - X_GROUPS, PACK)
+            if u == 0:
+                fid = fid_pool.tile([P, PACK, N_X], BF16)
+                fids[h] = fid
+            nc.scalar.activation(out=fids[h][:, u, :], in_=overlaps[n][:], func=ACT.Square)
+
+        def quantise_fidelity(h):
+            fid_grouped = fid_pool.tile([P, N_X, PACK], BF16, align_bytes=64)
+            nc.vector.tensor_copy(out=fid_grouped[:], in_=fids[h][:].rearrange("p u i -> p i u"))
+            nc.vector.quantize_mx(
+                out=fid_codes[:, h, :].bitcast(FP8X4),
+                scales=fid_scales[:, h, :],
+                in_=fid_grouped[:].rearrange("p i u -> p (i u)"),
+            )
+
+        def live(k):
+            return 0 <= k < QUARTERS
+
+        def last_of_group(k):
+            return live(k) and k % SLABS == SLABS - 1
+
+        for step in range(LOAD_LAG, QUARTERS + FIDELITY_QUANTISE_LAG):
+            if live(step - LOAD_LAG):
+                load(step - LOAD_LAG)
+            if live(step - QUANTISE_LAG):
+                copy_out(step - QUANTISE_LAG)
+            if live(step - SUBTRACT_LAG):
+                subtract_mean(step - SUBTRACT_LAG)
+            if last_of_group(step - NORM_LAG):
+                invert_norms((step - NORM_LAG) // SLABS)
+            if live(step - SQUARE_LAG):
+                sum_squares(step - SQUARE_LAG)
+            if live(step - SCALE_LAG):
+                scale(step - SCALE_LAG)
+            if live(step - QUANTISE_LAG):
+                quantise(step - QUANTISE_LAG)
+            if live(step - TURN_LAG):
+                turn(step - TURN_LAG)
+            if live(step - OVERLAP_LAG):
+                overlap_passes(step - OVERLAP_LAG)
+            if last_of_group(step - FIDELITY_LAG) and (step - FIDELITY_LAG) // SLABS >= X_GROUPS:
+                square_overlap((step - FIDELITY_LAG) // SLABS)
+            if last_of_group(step - FIDELITY_QUANTISE_LAG):
+                n = (step - FIDELITY_QUANTISE_LAG) // SLABS
+                if n >= X_GROUPS and (n - X_GROUPS) % PACK == PACK - 1:
+                    quantise_fidelity((n - X_GROUPS) // PACK)
+
+        for h in range(REF_PASSES):
+            nc.sync.dma_start(
+                out=w_words[:, h, :].bitcast(I32),
+                in_=components__words[h].rearrange("p n t -> p (n t)").bitcast(I32),
+            )
+            for quad in range(4):
+                nc.sync.dma_start(
+                    out=w_scales[32 * quad : 32 * quad + 4, h, :].bitcast(I32),
+                    in_=components__scales[h, 4 * quad : 4 * quad + 4, :].bitcast(I32),
+                )
+
+        projected = psum_small.tile([P, N_X // P, COMPONENTS], F32, tag="small")
+        for c in range(N_X // P):
+            cols = slice(P * c, P * (c + 1))
+            for h in range(REF_PASSES):
+                nc.tensor.matmul_mx(
+                    out=projected[:, c, :],
+                    lhsT=fid_codes[:, h, cols].bitcast(FP8X4),
+                    lhsT_scale=fid_scales[:, h, cols],
+                    rhs=w_words[:, h, :].bitcast(FP8X4),
+                    rhs_scale=w_scales[:, h, :],
+                    start=(h == 0),
+                    stop=(h == REF_PASSES - 1),
+                )
+        result = const.tile([P, N_X // P, COMPONENTS], F32)
+        nc.vector.tensor_copy(out=result[:], in_=projected[:])
+        nc.sync.dma_start(out=out.rearrange("(c p) n -> p c n", p=P), in_=result[:])

@@ -39,9 +39,10 @@ LOAD_LAG = -6
 SUBTRACT_LAG = 0
 SQUARE_LAG = SUBTRACT_LAG + 1
 NORM_LAG = SQUARE_LAG + 1
-SCALE_LAG = NORM_LAG + (SLABS - 1)
-TURN_LAG = SCALE_LAG + (SLABS - 1) + 1
-QUANTISE_LAG = TURN_LAG + 1
+SCALE_LAG = NORM_LAG + 1 + (SLABS - 1)
+TURN_LAG = SCALE_LAG + 1 + (SLABS - 1)
+COPY_LAG = TURN_LAG + 1
+QUANTISE_LAG = COPY_LAG + 1
 OVERLAP_LAG = QUANTISE_LAG + 1
 FIDELITY_LAG = OVERLAP_LAG + 1
 FIDELITY_QUANTISE_LAG = FIDELITY_LAG + 1
@@ -113,7 +114,7 @@ def tile_quantumkernelpca_kernel(tc, x, x_ref, mean_, components__words, compone
         rows_of = [x_groups[c] for c in range(X_GROUPS)]
         rows_of += [ref_groups[h, u] for h in range(REF_PASSES) for u in range(PACK)]
 
-        raws, diffs, units, sumsqs, invs, turneds, groupeds = {}, {}, {}, {}, {}, {}, {}
+        raws, diffs, units, sumsqs, norms, invs, turneds, groupeds = {}, {}, {}, {}, {}, {}, {}, {}
         codes_of, scales_of, overlaps, fids = {}, {}, {}, {}
 
         def load(k):
@@ -141,20 +142,22 @@ def tile_quantumkernelpca_kernel(tc, x, x_ref, mean_, components__words, compone
             squares = scratch.tile([P, SLAB_COLS], BF16)
             nc.scalar.activation(out=squares[:], in_=diffs[k][:], func=ACT.Square, accum_out=sumsqs[n][:, a : a + 1])
 
-        def invert_norms(n):
+        def take_norms(n):
             row_sumsq = psum_small.tile([P, SLABS], F32, tag="small")
             nc.tensor.matmul(
                 out=row_sumsq[:], lhsT=same_row[:].rearrange("p r t -> p (r t)"), rhs=sumsqs[n][:], start=True, stop=True
             )
             norm = stats.tile([P, SLABS], F32)
             nc.scalar.activation(out=norm[:], in_=row_sumsq[:], func=ACT.Sqrt)
-            inv = stats.tile([P, SLABS], F32)
-            nc.vector.tensor_scalar_add(out=inv[:], in0=norm[:], scalar1=EPS)
-            nc.vector.reciprocal(out=inv[:], in_=inv[:])
-            invs[n] = inv
+            norms[n] = norm
 
         def scale(k):
             n, a = divmod(k, SLABS)
+            if a == 0:
+                inv = stats.tile([P, SLABS], F32)
+                nc.vector.tensor_scalar_add(out=norms[n][:], in0=norms[n][:], scalar1=EPS)
+                invs[n] = inv
+            nc.vector.reciprocal(out=invs[n][:, a : a + 1], in_=norms[n][:, a : a + 1])
             unit = unit_pool.tile([P, SLAB_COLS], BF16)
             nc.gpsimd.tensor_scalar(
                 out=unit[:], in0=diffs[k][:], scalar1=invs[n][:, a : a + 1], scalar2=0.0, op0=ALU.mult, op1=ALU.add
@@ -176,7 +179,7 @@ def tile_quantumkernelpca_kernel(tc, x, x_ref, mean_, components__words, compone
                 grouped = grouped_pool.tile([P, PASSES_PER_BANK, K_PASS], BF16, align_bytes=64)
                 flat_out = grouped[:].rearrange("p i c -> p (i c)")
                 flat_in = turneds[k, b][:].rearrange("p i a c -> p (i a c)")
-                if k % 2 == 1 and b == 1:
+                if b == 1:
                     nc.vector.tensor_copy(out=flat_out, in_=flat_in)
                 else:
                     nc.scalar.copy(out=flat_out, in_=flat_in)
@@ -245,17 +248,17 @@ def tile_quantumkernelpca_kernel(tc, x, x_ref, mean_, components__words, compone
             if live(step - LOAD_LAG):
                 load(step - LOAD_LAG)
             if live(step - QUANTISE_LAG):
-                copy_out(step - QUANTISE_LAG)
+                quantise(step - QUANTISE_LAG)
+            if live(step - SCALE_LAG):
+                scale(step - SCALE_LAG)
+            if live(step - COPY_LAG):
+                copy_out(step - COPY_LAG)
             if live(step - SUBTRACT_LAG):
                 subtract_mean(step - SUBTRACT_LAG)
             if last_of_group(step - NORM_LAG):
-                invert_norms((step - NORM_LAG) // SLABS)
+                take_norms((step - NORM_LAG) // SLABS)
             if live(step - SQUARE_LAG):
                 sum_squares(step - SQUARE_LAG)
-            if live(step - SCALE_LAG):
-                scale(step - SCALE_LAG)
-            if live(step - QUANTISE_LAG):
-                quantise(step - QUANTISE_LAG)
             if live(step - TURN_LAG):
                 turn(step - TURN_LAG)
             if live(step - OVERLAP_LAG):

@@ -164,15 +164,14 @@ def tile_quantumkernelpca_kernel(tc, x, x_ref, mean_, components__words, compone
             )
             units[k] = unit
 
-        def turn(k):
+        def turn(k, b):
             n, c = divmod(k, SLABS)
-            for b in range(QUARTER_BANKS):
-                turned = psum_turn.tile([P, PASSES_PER_BANK, SLABS, P], BF16)
-                for i in range(PASSES_PER_BANK):
-                    g = QUARTER_PASSES * c + PASSES_PER_BANK * b + i
-                    for a in range(SLABS):
-                        nc.tensor.transpose(turned[:, i, a, :], units[SLABS * n + a][:, P * g : P * (g + 1)], ident[:])
-                turneds[k, b] = turned
+            turned = psum_turn.tile([P, PASSES_PER_BANK, SLABS, P], BF16)
+            for i in range(PASSES_PER_BANK):
+                g = QUARTER_PASSES * c + PASSES_PER_BANK * b + i
+                for a in range(SLABS):
+                    nc.tensor.transpose(turned[:, i, a, :], units[SLABS * n + a][:, P * g : P * (g + 1)], ident[:])
+            turneds[k, b] = turned
 
         def copy_out(k):
             for b in range(QUARTER_BANKS):
@@ -204,14 +203,15 @@ def tile_quantumkernelpca_kernel(tc, x, x_ref, mean_, components__words, compone
                         out=codes_of[n][:, g, :].bitcast(FP8X4), scales=scales_of[n][:, g, :], in_=groupeds[k, b][:, i, :]
                     )
 
-        def overlap_passes(k):
+        def overlap_passes(k, b):
             n, c = divmod(k, SLABS)
             if n < X_GROUPS:
                 return
-            if c == 0:
+            if c == 0 and b == 0:
                 overlap = psum_ov.tile([P, N_X], F32)
                 overlaps[n] = overlap
-            for g in range(QUARTER_PASSES * c, QUARTER_PASSES * (c + 1)):
+            first = QUARTER_PASSES * c + PASSES_PER_BANK * b
+            for g in range(first, first + PASSES_PER_BANK):
                 nc.tensor.matmul_mx(
                     out=overlaps[n][:],
                     lhsT=codes_of[n][:, g, :].bitcast(FP8X4),
@@ -259,10 +259,11 @@ def tile_quantumkernelpca_kernel(tc, x, x_ref, mean_, components__words, compone
                 take_norms((step - NORM_LAG) // SLABS)
             if live(step - SQUARE_LAG):
                 sum_squares(step - SQUARE_LAG)
-            if live(step - TURN_LAG):
-                turn(step - TURN_LAG)
-            if live(step - OVERLAP_LAG):
-                overlap_passes(step - OVERLAP_LAG)
+            for b in range(QUARTER_BANKS):
+                if live(step - TURN_LAG):
+                    turn(step - TURN_LAG, b)
+                if live(step - OVERLAP_LAG):
+                    overlap_passes(step - OVERLAP_LAG, b)
             if last_of_group(step - FIDELITY_LAG) and (step - FIDELITY_LAG) // SLABS >= X_GROUPS:
                 square_overlap((step - FIDELITY_LAG) // SLABS)
             if last_of_group(step - FIDELITY_QUANTISE_LAG):

@@ -28,7 +28,10 @@ SLAB_ROWS = P // PACK
 SLAB_COLS = FEATURES // PACK
 SLABS = P // SLAB_ROWS
 BANK_BF16 = 1024
+BANK_F32 = 512
 PASSES_PER_BANK = BANK_BF16 // K_PASS
+RUN = 256
+PAIR = 2
 GROUPS = (N_X + N_REF) // P
 X_GROUPS = N_X // P
 QUARTERS = GROUPS * SLABS
@@ -68,7 +71,7 @@ def tile_quantumkernelpca_kernel(tc, x, x_ref, mean_, components__words, compone
         psum_small = ctx.enter_context(tc.psum_pool(name="psum_small", bufs=1))
         ctx.enter_context(tc.manual_schedule())
 
-        ident = const.tile([P, P], BF16)
+        ident = const.tile([P, P], F32)
         make_identity(nc, ident[:])
         warm = const.tile([P, 1], F32)
         nc.vector.memset(warm[:], 1.0)
@@ -85,8 +88,8 @@ def tile_quantumkernelpca_kernel(tc, x, x_ref, mean_, components__words, compone
         mean_rows = const.tile([P, SLAB_COLS], BF16)
         nc.vector.memset(mean_rows[:].bitcast(I32), 0)
         nc.sync.dma_start(
-            out=mean_rows[0:PACK, :].rearrange("t (g j) -> t g j", j=P),
-            in_=mean_.rearrange("(g t j) -> t g j", t=PACK, j=P),
+            out=mean_rows[0:PACK, :].rearrange("t (s i) -> t s i", i=RUN),
+            in_=mean_.rearrange("(s t i) -> t s i", t=PACK, i=RUN),
         )
         mean_lo = psum_mean.tile([P, BANK_BF16], BF16)
         mean_hi = psum_mean.tile([P, BANK_BF16], BF16)
@@ -109,8 +112,8 @@ def tile_quantumkernelpca_kernel(tc, x, x_ref, mean_, components__words, compone
         fid_codes = const.tile([P, REF_PASSES, N_X], U32, align_bytes=64)
         fid_scales = const.tile([P, REF_PASSES, N_X], U8, align_bytes=64)
 
-        x_groups = x.rearrange("(c q) (g t j) -> c t q g j", q=P, t=PACK, j=P)
-        ref_groups = x_ref.rearrange("(h q u) (g t j) -> h u t q g j", q=P, u=PACK, t=PACK, j=P)
+        x_groups = x.rearrange("(c q) (s t i) -> c t q s i", q=P, t=PACK, i=RUN)
+        ref_groups = x_ref.rearrange("(h q u) (s t i) -> h u t q s i", q=P, u=PACK, t=PACK, i=RUN)
         rows_of = [x_groups[c] for c in range(X_GROUPS)]
         rows_of += [ref_groups[h, u] for h in range(REF_PASSES) for u in range(PACK)]
 
@@ -122,7 +125,7 @@ def tile_quantumkernelpca_kernel(tc, x, x_ref, mean_, components__words, compone
             raw = raw_pool.tile([P, SLAB_COLS], BF16)
             for t in range(PACK):
                 nc.sync.dma_start(
-                    out=raw[t:P:PACK, :].rearrange("r (g j) -> r g j", j=P),
+                    out=raw[t:P:PACK, :].rearrange("r (s i) -> r s i", i=RUN),
                     in_=rows_of[n][t, SLAB_ROWS * a : SLAB_ROWS * (a + 1)],
                 )
             raws[k] = raw
@@ -166,19 +169,19 @@ def tile_quantumkernelpca_kernel(tc, x, x_ref, mean_, components__words, compone
 
         def turn(k, b):
             n, c = divmod(k, SLABS)
-            turned = psum_turn.tile([P, PASSES_PER_BANK, SLABS, P], BF16)
-            for i in range(PASSES_PER_BANK):
-                g = QUARTER_PASSES * c + PASSES_PER_BANK * b + i
-                for a in range(SLABS):
-                    nc.tensor.transpose(turned[:, i, a, :], units[SLABS * n + a][:, P * g : P * (g + 1)], ident[:])
+            span = QUARTER_BANKS * c + b
+            turned = psum_turn.tile([P, BANK_F32], F32)
+            for a in range(SLABS):
+                words = units[SLABS * n + a][:].bitcast(F32)
+                nc.tensor.transpose(turned[:, P * a : P * (a + 1)], words[:, P * span : P * (span + 1)], ident[:])
             turneds[k, b] = turned
 
         def copy_out(k):
             for b in range(QUARTER_BANKS):
                 grouped = grouped_pool.tile([P, PASSES_PER_BANK, K_PASS], BF16, align_bytes=64)
-                flat_out = grouped[:].rearrange("p i c -> p (i c)")
-                flat_in = turneds[k, b][:].rearrange("p i a c -> p (i a c)")
-                if b == 1:
+                flat_out = grouped[:].bitcast(F32).rearrange("p w (q v) -> p w q v", v=PAIR)
+                flat_in = turneds[k, b][:].rearrange("p (q w v) -> p w q v", w=PASSES_PER_BANK, v=PAIR)
+                if b == 1 and k % 2 == 1:
                     nc.vector.tensor_copy(out=flat_out, in_=flat_in)
                 else:
                     nc.scalar.copy(out=flat_out, in_=flat_in)

@@ -29,26 +29,22 @@ SLAB_COLS = FEATURES // PACK
 SLABS = P // SLAB_ROWS
 BANK_BF16 = 1024
 BANK_F32 = 512
-PASSES_PER_BANK = BANK_BF16 // K_PASS
 RUN = 256
 PAIR = 2
+SPANS = SLAB_COLS // RUN
+SPAN_PASSES = PASSES // SPANS
+HALF_SPANS = SPANS // 2
+QUARTER_SPANS = 2
+QUARTER_PASSES = QUARTER_SPANS * SPAN_PASSES
 GROUPS = (N_X + N_REF) // P
 X_GROUPS = N_X // P
-QUARTERS = GROUPS * SLABS
-QUARTER_PASSES = PASSES // SLABS
-QUARTER_BANKS = QUARTER_PASSES // PASSES_PER_BANK
-
-LOAD_LAG = -6
-SUBTRACT_LAG = 0
-SQUARE_LAG = SUBTRACT_LAG + 1
-NORM_LAG = SQUARE_LAG + 1
-SCALE_LAG = NORM_LAG + 1 + (SLABS - 1)
-TURN_LAG = SCALE_LAG + 1 + (SLABS - 1)
-COPY_LAG = TURN_LAG + 1
-QUANTISE_LAG = COPY_LAG + 1
-OVERLAP_LAG = QUANTISE_LAG + 1
-FIDELITY_LAG = OVERLAP_LAG + 1
-FIDELITY_QUANTISE_LAG = FIDELITY_LAG + 1
+HALF = N_X // 2
+SLAB_COUNT = GROUPS * SLABS
+TOGETHER = 2
+LOAD_AHEAD = 6
+MEAN_TAGS = ("mean_lo", "mean_hi")
+DRAIN_BANKS = 5
+RELIEVED_GROUPS = (X_GROUPS + 1, X_GROUPS + 3)
 
 FLOPS = 2 * N_X * N_REF * FEATURES + 2 * N_X * N_REF * COMPONENTS
 
@@ -62,51 +58,60 @@ def tile_quantumkernelpca_kernel(tc, x, x_ref, mean_, components__words, compone
         unit_pool = ctx.enter_context(tc.tile_pool(name="unit", bufs=8))
         scratch = ctx.enter_context(tc.tile_pool(name="scratch", bufs=1))
         stats = ctx.enter_context(tc.tile_pool(name="stats", bufs=3))
+        inv_pool = ctx.enter_context(tc.tile_pool(name="inv", bufs=8))
         grouped_pool = ctx.enter_context(tc.tile_pool(name="grouped", bufs=4))
         ref_pool = ctx.enter_context(tc.tile_pool(name="ref", bufs=2))
         fid_pool = ctx.enter_context(tc.tile_pool(name="fid", bufs=2))
+        result_pool = ctx.enter_context(tc.tile_pool(name="result", bufs=2))
         psum_mean = ctx.enter_context(tc.psum_pool(name="psum_mean", bufs=1))
         psum_turn = ctx.enter_context(tc.psum_pool(name="psum_turn", bufs=3))
         psum_ov = ctx.enter_context(tc.psum_pool(name="psum_ov", bufs=2))
         psum_small = ctx.enter_context(tc.psum_pool(name="psum_small", bufs=1))
         ctx.enter_context(tc.manual_schedule())
 
+        mean_rows = const.tile([P, RUN], BF16)
+        nc.gpsimd.memset(mean_rows[:].bitcast(I32), 0)
+        nc.scalar.dma_start(
+            out=mean_rows[0 : SPANS * PACK, :], in_=mean_.rearrange("(s t i) -> (s t) i", t=PACK, i=RUN)
+        )
         ident = const.tile([P, P], F32)
         make_identity(nc, ident[:])
+        pick = const.tile([P, SPANS, SLAB_ROWS, PACK], BF16)
+        nc.vector.tensor_copy(
+            out=pick[:],
+            in_=ident[:, 0 : SPANS * PACK]
+            .rearrange("p (s t) -> p s t", t=PACK)
+            .unsqueeze(2)
+            .to_broadcast([P, SPANS, SLAB_ROWS, PACK]),
+        )
+        picks = pick[:].rearrange("p s r t -> p (s r t)")
+
+        mean_lo = psum_mean.tile([P, BANK_BF16], BF16, tag=MEAN_TAGS[0])
+        mean_hi = psum_mean.tile([P, BANK_BF16], BF16, tag=MEAN_TAGS[1])
+        mean_banks = [mean_lo, mean_hi]
+        for s in range(SPANS):
+            h, j = divmod(s, SPANS // 2)
+            nc.tensor.matmul(
+                out=mean_banks[h][:, RUN * j : RUN * (j + 1)],
+                lhsT=picks[:, P * s : P * (s + 1)],
+                rhs=mean_rows[:],
+                start=True,
+                stop=True,
+            )
+
         warm = const.tile([P, 1], F32)
         nc.vector.memset(warm[:], 1.0)
         nc.scalar.activation(out=warm[:], in_=warm[:], func=ACT.Sqrt)
-        pick = const.tile([P, SLAB_ROWS, PACK], BF16)
-        nc.vector.tensor_copy(out=pick[:], in_=ident[:, 0:PACK].unsqueeze(1).to_broadcast([P, SLAB_ROWS, PACK]))
         row_of = const.tile([P, SLAB_ROWS], F32)
         nc.vector.tensor_reduce(
             out=row_of[:], in_=ident[:].rearrange("p (r t) -> p r t", t=PACK), axis=AXIS.X, op=ALU.add
         )
         same_row = const.tile([P, SLAB_ROWS, PACK], F32)
-        nc.vector.tensor_copy(out=same_row[:], in_=row_of[:].unsqueeze(2).to_broadcast([P, SLAB_ROWS, PACK]))
-
-        mean_rows = const.tile([P, SLAB_COLS], BF16)
-        nc.vector.memset(mean_rows[:].bitcast(I32), 0)
-        nc.sync.dma_start(
-            out=mean_rows[0:PACK, :].rearrange("t (s i) -> t s i", i=RUN),
-            in_=mean_.rearrange("(s t i) -> t s i", t=PACK, i=RUN),
-        )
-        mean_lo = psum_mean.tile([P, BANK_BF16], BF16)
-        mean_hi = psum_mean.tile([P, BANK_BF16], BF16)
-        mean_banks = [mean_lo, mean_hi]
-        for h in range(2):
-            for c in range(2):
-                nc.tensor.matmul(
-                    out=mean_banks[h][:, 512 * c : 512 * (c + 1)],
-                    lhsT=pick[:].rearrange("p r t -> p (r t)"),
-                    rhs=mean_rows[:, BANK_BF16 * h + 512 * c : BANK_BF16 * h + 512 * (c + 1)],
-                    start=True,
-                    stop=True,
-                )
 
         w_words = const.tile([P, REF_PASSES, COMPONENTS], U32, align_bytes=64)
         w_scales = const.tile([P, REF_PASSES, COMPONENTS], U8, align_bytes=64)
         nc.vector.memset(w_scales[:].rearrange("p h n -> p (h n)").bitcast(I32), 0)
+        nc.vector.tensor_copy(out=same_row[:], in_=row_of[:].unsqueeze(2).to_broadcast([P, SLAB_ROWS, PACK]))
         x_codes = const.tile([P, PASSES, N_X], U32, align_bytes=64)
         x_scales = const.tile([P, PASSES, N_X], U8, align_bytes=64)
         fid_codes = const.tile([P, REF_PASSES, N_X], U32, align_bytes=64)
@@ -117,17 +122,22 @@ def tile_quantumkernelpca_kernel(tc, x, x_ref, mean_, components__words, compone
         rows_of = [x_groups[c] for c in range(X_GROUPS)]
         rows_of += [ref_groups[h, u] for h in range(REF_PASSES) for u in range(PACK)]
 
-        raws, diffs, units, sumsqs, norms, invs, turneds, groupeds = {}, {}, {}, {}, {}, {}, {}, {}
-        codes_of, scales_of, overlaps, fids = {}, {}, {}, {}
+        raws, diffs, sumsqs, norms, invs, units = {}, {}, {}, {}, {}, {}
+        turneds, groupeds, codes_of, scales_of = {}, {}, {}, {}
+        overlaps, fids, fid_groupeds = {}, {}, {}
+        drained = []
 
         def load(k):
+            if k >= SLAB_COUNT:
+                return
             n, a = divmod(k, SLABS)
             raw = raw_pool.tile([P, SLAB_COLS], BF16)
-            for t in range(PACK):
-                nc.sync.dma_start(
-                    out=raw[t:P:PACK, :].rearrange("r (s i) -> r s i", i=RUN),
-                    in_=rows_of[n][t, SLAB_ROWS * a : SLAB_ROWS * (a + 1)],
-                )
+            for spans in [range(0, SPANS // 2), range(SPANS // 2, SPANS)] if k == 0 else [range(SPANS)]:
+                for t in range(PACK):
+                    nc.sync.dma_start(
+                        out=raw[t:P:PACK, RUN * spans.start : RUN * spans.stop].rearrange("r (s i) -> r s i", i=RUN),
+                        in_=rows_of[n][t, SLAB_ROWS * a : SLAB_ROWS * (a + 1), spans.start : spans.stop],
+                    )
             raws[k] = raw
 
         def subtract_mean(k):
@@ -145,51 +155,75 @@ def tile_quantumkernelpca_kernel(tc, x, x_ref, mean_, components__words, compone
             squares = scratch.tile([P, SLAB_COLS], BF16)
             nc.scalar.activation(out=squares[:], in_=diffs[k][:], func=ACT.Square, accum_out=sumsqs[n][:, a : a + 1])
 
-        def take_norms(n):
-            row_sumsq = psum_small.tile([P, SLABS], F32, tag="small")
-            nc.tensor.matmul(
-                out=row_sumsq[:], lhsT=same_row[:].rearrange("p r t -> p (r t)"), rhs=sumsqs[n][:], start=True, stop=True
-            )
-            norm = stats.tile([P, SLABS], F32)
-            nc.scalar.activation(out=norm[:], in_=row_sumsq[:], func=ACT.Sqrt)
-            norms[n] = norm
-
-        def scale(k):
+        def take_norms(k):
             n, a = divmod(k, SLABS)
-            if a == 0:
-                inv = stats.tile([P, SLABS], F32)
-                nc.vector.tensor_scalar_add(out=norms[n][:], in0=norms[n][:], scalar1=EPS)
-                invs[n] = inv
-            nc.vector.reciprocal(out=invs[n][:, a : a + 1], in_=norms[n][:, a : a + 1])
+            row_sumsq = psum_small.tile([P, TOGETHER], F32, tag="small")
+            nc.tensor.matmul(
+                out=row_sumsq[:],
+                lhsT=same_row[:].rearrange("p r t -> p (r t)"),
+                rhs=sumsqs[n][:, a : a + TOGETHER],
+                start=True,
+                stop=True,
+            )
+            norm = stats.tile([P, TOGETHER], F32)
+            nc.scalar.activation(out=norm[:], in_=row_sumsq[:], func=ACT.Sqrt)
+            norms[k] = norm
+
+        def add_epsilon(k):
+            nc.vector.tensor_scalar_add(out=norms[k][:], in0=norms[k][:], scalar1=EPS)
+
+        def invert_norms(k):
+            inv = inv_pool.tile([P, TOGETHER], F32)
+            nc.vector.reciprocal(out=inv[:], in_=norms[k][:])
+            for i in range(TOGETHER):
+                invs[k + i] = inv[:, i : i + 1]
+
+        def scale_on_gpsimd(k):
             unit = unit_pool.tile([P, SLAB_COLS], BF16)
             nc.gpsimd.tensor_scalar(
-                out=unit[:], in0=diffs[k][:], scalar1=invs[n][:, a : a + 1], scalar2=0.0, op0=ALU.mult, op1=ALU.add
+                out=unit[:], in0=diffs[k][:], scalar1=invs[k], scalar2=0.0, op0=ALU.mult, op1=ALU.add
             )
             units[k] = unit
 
-        def turn(k, b):
-            n, c = divmod(k, SLABS)
-            span = QUARTER_BANKS * c + b
-            turned = psum_turn.tile([P, BANK_F32], F32)
+        def scale_on_vector(k):
+            unit = unit_pool.tile([P, SLAB_COLS], BF16)
+            nc.vector.tensor_scalar_mul(out=unit[:], in0=diffs[k][:], scalar1=invs[k])
+            units[k] = unit
+
+        def turn_into(turned, n, span):
             for a in range(SLABS):
                 words = units[SLABS * n + a][:].bitcast(F32)
                 nc.tensor.transpose(turned[:, P * a : P * (a + 1)], words[:, P * span : P * (span + 1)], ident[:])
-            turneds[k, b] = turned
+            turneds[n, span] = turned
 
-        def copy_out(k):
-            for b in range(QUARTER_BANKS):
-                grouped = grouped_pool.tile([P, PASSES_PER_BANK, K_PASS], BF16, align_bytes=64)
-                flat_out = grouped[:].bitcast(F32).rearrange("p w (q v) -> p w q v", v=PAIR)
-                flat_in = turneds[k, b][:].rearrange("p (q w v) -> p w q v", w=PASSES_PER_BANK, v=PAIR)
-                if b == 1 and k % 2 == 1:
-                    nc.vector.tensor_copy(out=flat_out, in_=flat_in)
-                else:
-                    nc.scalar.copy(out=flat_out, in_=flat_in)
-                groupeds[k, b] = grouped
+        def turn(n, span):
+            turned = psum_turn.tile([P, BANK_F32], F32)
+            turn_into(turned, n, span)
 
-        def quantise(k):
-            n, c = divmod(k, SLABS)
-            if c == 0:
+        def turn_in_drain(n, span):
+            drained.append((n, span))
+            place = len(drained) % DRAIN_BANKS
+            if place < len(MEAN_TAGS):
+                late_turned = psum_mean.tile([P, BANK_F32], F32, tag=MEAN_TAGS[place])
+                turn_into(late_turned, n, span)
+            else:
+                turn(n, span)
+
+        def empty(n, span, by_vector):
+            quarter, b = divmod(span, QUARTER_SPANS)
+            if (n, quarter) not in groupeds:
+                grouped = grouped_pool.tile([P, QUARTER_PASSES, K_PASS], BF16, align_bytes=64)
+                groupeds[n, quarter] = grouped
+            passes = slice(SPAN_PASSES * b, SPAN_PASSES * (b + 1))
+            words_out = groupeds[n, quarter][:, passes, :].bitcast(F32).rearrange("p w (q v) -> p w q v", v=PAIR)
+            words_in = turneds[n, span][:].rearrange("p (q w v) -> p w q v", w=SPAN_PASSES, v=PAIR)
+            if by_vector:
+                nc.vector.tensor_copy(out=words_out, in_=words_in)
+            else:
+                nc.scalar.copy(out=words_out, in_=words_in)
+
+        def quantise(n, passes):
+            if n not in codes_of:
                 if n < X_GROUPS:
                     cols = slice(P * n, P * (n + 1))
                     codes_of[n] = x_codes[:, :, cols]
@@ -199,105 +233,217 @@ def tile_quantumkernelpca_kernel(tc, x, x_ref, mean_, components__words, compone
                     ref_scales = ref_pool.tile([P, PASSES, P], U8, align_bytes=64)
                     codes_of[n] = ref_codes[:]
                     scales_of[n] = ref_scales[:]
-            for b in range(QUARTER_BANKS):
-                for i in range(PASSES_PER_BANK):
-                    g = QUARTER_PASSES * c + PASSES_PER_BANK * b + i
-                    nc.vector.quantize_mx(
-                        out=codes_of[n][:, g, :].bitcast(FP8X4), scales=scales_of[n][:, g, :], in_=groupeds[k, b][:, i, :]
-                    )
+            width = 1 if n < X_GROUPS else len(passes)
+            for g in passes if n < X_GROUPS else passes[:1]:
+                quarter, i = divmod(g, QUARTER_PASSES)
+                nc.vector.quantize_mx(
+                    out=codes_of[n][:, g : g + width, :].rearrange("p g c -> p (g c)").bitcast(FP8X4),
+                    scales=scales_of[n][:, g : g + width, :].rearrange("p g c -> p (g c)"),
+                    in_=groupeds[n, quarter][:, i : i + width, :].rearrange("p w c -> p (w c)"),
+                )
 
-        def overlap_passes(k, b):
-            n, c = divmod(k, SLABS)
+        def passes_of(span, count=1):
+            return range(SPAN_PASSES * span, SPAN_PASSES * (span + count))
+
+        def overlap_passes(n, span, count=1, half=None):
             if n < X_GROUPS:
                 return
-            if c == 0 and b == 0:
-                overlap = psum_ov.tile([P, N_X], F32)
-                overlaps[n] = overlap
-            first = QUARTER_PASSES * c + PASSES_PER_BANK * b
-            for g in range(first, first + PASSES_PER_BANK):
+            cols = slice(0, N_X) if half is None else slice(half * HALF, (half + 1) * HALF)
+            for g in passes_of(span, count):
+                if g == 0:
+                    overlap = psum_ov.tile([P, N_X], F32)
+                    overlaps[n, half] = overlap
                 nc.tensor.matmul_mx(
-                    out=overlaps[n][:],
+                    out=overlaps[n, half][:, 0 : cols.stop - cols.start],
                     lhsT=codes_of[n][:, g, :].bitcast(FP8X4),
                     lhsT_scale=scales_of[n][:, g, :],
-                    rhs=x_codes[:, g, :].bitcast(FP8X4),
-                    rhs_scale=x_scales[:, g, :],
+                    rhs=x_codes[:, g, cols].bitcast(FP8X4),
+                    rhs_scale=x_scales[:, g, cols],
                     start=(g == 0),
                     stop=(g == PASSES - 1),
                 )
 
-        def square_overlap(n):
+        def square_overlap(n, half=None):
+            if n < X_GROUPS:
+                return
             h, u = divmod(n - X_GROUPS, PACK)
             if u == 0:
                 fid = fid_pool.tile([P, PACK, N_X], BF16)
                 fids[h] = fid
-            nc.scalar.activation(out=fids[h][:, u, :], in_=overlaps[n][:], func=ACT.Square)
+            cols = slice(0, N_X) if half is None else slice(half * HALF, (half + 1) * HALF)
+            nc.scalar.activation(
+                out=fids[h][:, u, cols], in_=overlaps[n, half][:, 0 : cols.stop - cols.start], func=ACT.Square
+            )
 
-        def quantise_fidelity(h):
-            fid_grouped = fid_pool.tile([P, N_X, PACK], BF16, align_bytes=64)
-            nc.vector.tensor_copy(out=fid_grouped[:], in_=fids[h][:].rearrange("p u i -> p i u"))
+        def group_fidelity(h, half):
+            cols = slice(half * HALF, (half + 1) * HALF)
+            fid_grouped = fid_pool.tile([P, HALF, PACK], BF16, align_bytes=64)
+            nc.vector.tensor_copy(
+                out=fid_grouped[:].rearrange("p (c i) u -> p c u i", i=PACK),
+                in_=fids[h][:, :, cols].rearrange("p u (c i) -> p c u i", i=PACK),
+            )
+            fid_groupeds[h, half] = fid_grouped
+
+        def quantise_fidelity(h, half):
+            cols = slice(half * HALF, (half + 1) * HALF)
             nc.vector.quantize_mx(
-                out=fid_codes[:, h, :].bitcast(FP8X4),
-                scales=fid_scales[:, h, :],
-                in_=fid_grouped[:].rearrange("p i u -> p (i u)"),
+                out=fid_codes[:, h, cols].bitcast(FP8X4),
+                scales=fid_scales[:, h, cols],
+                in_=fid_groupeds[h, half][:].rearrange("p i u -> p (i u)"),
             )
 
-        def live(k):
-            return 0 <= k < QUARTERS
-
-        def last_of_group(k):
-            return live(k) and k % SLABS == SLABS - 1
-
-        for step in range(LOAD_LAG, QUARTERS + FIDELITY_QUANTISE_LAG):
-            if live(step - LOAD_LAG):
-                load(step - LOAD_LAG)
-            if live(step - QUANTISE_LAG):
-                quantise(step - QUANTISE_LAG)
-            if live(step - SCALE_LAG):
-                scale(step - SCALE_LAG)
-            if live(step - COPY_LAG):
-                copy_out(step - COPY_LAG)
-            if live(step - SUBTRACT_LAG):
-                subtract_mean(step - SUBTRACT_LAG)
-            if last_of_group(step - NORM_LAG):
-                take_norms((step - NORM_LAG) // SLABS)
-            if live(step - SQUARE_LAG):
-                sum_squares(step - SQUARE_LAG)
-            for b in range(QUARTER_BANKS):
-                if live(step - TURN_LAG):
-                    turn(step - TURN_LAG, b)
-                if live(step - OVERLAP_LAG):
-                    overlap_passes(step - OVERLAP_LAG, b)
-            if last_of_group(step - FIDELITY_LAG) and (step - FIDELITY_LAG) // SLABS >= X_GROUPS:
-                square_overlap((step - FIDELITY_LAG) // SLABS)
-            if last_of_group(step - FIDELITY_QUANTISE_LAG):
-                n = (step - FIDELITY_QUANTISE_LAG) // SLABS
-                if n >= X_GROUPS and (n - X_GROUPS) % PACK == PACK - 1:
-                    quantise_fidelity((n - X_GROUPS) // PACK)
-
-        for h in range(REF_PASSES):
-            nc.sync.dma_start(
-                out=w_words[:, h, :].bitcast(I32),
-                in_=components__words[h].rearrange("p n t -> p (n t)").bitcast(I32),
-            )
-            for quad in range(4):
-                nc.sync.dma_start(
-                    out=w_scales[32 * quad : 32 * quad + 4, h, :].bitcast(I32),
-                    in_=components__scales[h, 4 * quad : 4 * quad + 4, :].bitcast(I32),
-                )
-
-        projected = psum_small.tile([P, N_X // P, COMPONENTS], F32, tag="small")
-        for c in range(N_X // P):
-            cols = slice(P * c, P * (c + 1))
+        def load_weight():
             for h in range(REF_PASSES):
-                nc.tensor.matmul_mx(
-                    out=projected[:, c, :],
-                    lhsT=fid_codes[:, h, cols].bitcast(FP8X4),
-                    lhsT_scale=fid_scales[:, h, cols],
-                    rhs=w_words[:, h, :].bitcast(FP8X4),
-                    rhs_scale=w_scales[:, h, :],
-                    start=(h == 0),
-                    stop=(h == REF_PASSES - 1),
+                nc.sync.dma_start(
+                    out=w_words[:, h, :].bitcast(I32),
+                    in_=components__words[h].rearrange("p n t -> p (n t)").bitcast(I32),
                 )
-        result = const.tile([P, N_X // P, COMPONENTS], F32)
-        nc.vector.tensor_copy(out=result[:], in_=projected[:])
-        nc.sync.dma_start(out=out.rearrange("(c p) n -> p c n", p=P), in_=result[:])
+                for quad in range(4):
+                    nc.sync.dma_start(
+                        out=w_scales[32 * quad : 32 * quad + 4, h, :].bitcast(I32),
+                        in_=components__scales[h, 4 * quad : 4 * quad + 4, :].bitcast(I32),
+                    )
+
+        def project(half):
+            blocks = HALF // P
+            projected = psum_small.tile([P, blocks, COMPONENTS], F32, tag="small")
+            for i in range(blocks):
+                block = blocks * half + i
+                cols = slice(P * block, P * (block + 1))
+                for h in range(REF_PASSES):
+                    nc.tensor.matmul_mx(
+                        out=projected[:, i, :],
+                        lhsT=fid_codes[:, h, cols].bitcast(FP8X4),
+                        lhsT_scale=fid_scales[:, h, cols],
+                        rhs=w_words[:, h, :].bitcast(FP8X4),
+                        rhs_scale=w_scales[:, h, :],
+                        start=(h == 0),
+                        stop=(h == REF_PASSES - 1),
+                    )
+            result = result_pool.tile([P, blocks, COMPONENTS], F32)
+            nc.vector.tensor_copy(out=result[:], in_=projected[:])
+            nc.sync.dma_start(
+                out=out.rearrange("(c p) n -> p c n", p=P)[:, blocks * half : blocks * (half + 1), :], in_=result[:]
+            )
+
+        for k in range(LOAD_AHEAD):
+            load(k)
+        for k in range(0, SLAB_COUNT, TOGETHER):
+            scaled = k - 4
+            turned_group, turned_half = divmod(k // TOGETHER - 4, 2)
+            coded_group, coded_half = divmod(k // TOGETHER - 5, 2)
+            t0 = HALF_SPANS * turned_half
+            c0 = HALF_SPANS * coded_half
+
+            if scaled >= 0:
+                add_epsilon(scaled)
+            load(k + LOAD_AHEAD)
+            if turned_group >= 0:
+                for span in range(t0, t0 + 3):
+                    turn(turned_group, span)
+            if coded_group >= 0:
+                last_call = 1 if coded_group < X_GROUPS else QUARTER_PASSES
+                early = passes_of(c0, QUARTER_SPANS)
+                quantise(coded_group, passes_of(c0 + QUARTER_SPANS, QUARTER_SPANS))
+                quantise(coded_group, range(early.start, early.stop - last_call))
+            if scaled >= 0:
+                invert_norms(scaled)
+            if coded_group >= 0:
+                quantise(coded_group, range(early.stop - last_call, early.stop))
+            if scaled >= 0:
+                scale_on_gpsimd(scaled)
+                scale_on_gpsimd(scaled + 1)
+            if turned_group >= 0:
+                empty(turned_group, t0, by_vector=True)
+            if k > 0:
+                sum_squares(k - 1)
+            subtract_mean(k)
+            if turned_group >= 0:
+                empty(turned_group, t0 + 1, by_vector=False)
+            if coded_group >= 0:
+                overlap_passes(coded_group, c0)
+            if turned_group >= 0:
+                empty(turned_group, t0 + 2, by_vector=False)
+                turn(turned_group, t0 + 3)
+                empty(turned_group, t0 + 3, by_vector=turned_group in RELIEVED_GROUPS and turned_half == 1)
+            if k >= 2:
+                take_norms(k - 2)
+            if coded_group >= 0:
+                overlap_passes(coded_group, c0 + 1)
+            load(k + 1 + LOAD_AHEAD)
+            if coded_group >= 0:
+                overlap_passes(coded_group, c0 + 2, count=2)
+            sum_squares(k)
+            subtract_mean(k + 1)
+            if coded_group >= 0 and coded_half == 1:
+                square_overlap(coded_group)
+        load_weight()
+
+        ninth, tenth, last = GROUPS - 3, GROUPS - 2, GROUPS - 1
+        first, third = SLABS * last, SLABS * last + 2
+        add_epsilon(first)
+        invert_norms(first)
+        for span in range(3):
+            turn(tenth, span)
+        quantise(ninth, passes_of(6, QUARTER_SPANS))
+        quantise(ninth, passes_of(4, QUARTER_SPANS))
+        scale_on_gpsimd(first)
+        overlap_passes(ninth, 4, count=2)
+        sum_squares(third + 1)
+        for span in range(3):
+            empty(tenth, span, by_vector=True)
+        for span in range(3):
+            quantise(tenth, passes_of(span))
+        scale_on_vector(first + 1)
+        turn(tenth, 3)
+        turn_in_drain(tenth, 4)
+        turn_in_drain(tenth, 5)
+        empty(tenth, 3, by_vector=False)
+        take_norms(third)
+        overlap_passes(ninth, 6, count=2)
+        empty(tenth, 4, by_vector=False)
+        add_epsilon(third)
+        quantise(tenth, passes_of(3))
+        empty(tenth, 5, by_vector=False)
+        invert_norms(third)
+        square_overlap(ninth)
+        scale_on_vector(third)
+        overlap_passes(tenth, 0, count=3)
+        turn_in_drain(tenth, 6)
+        turn_in_drain(tenth, 7)
+        overlap_passes(tenth, 3)
+        empty(tenth, 6, by_vector=False)
+        empty(tenth, 7, by_vector=False)
+        scale_on_vector(third + 1)
+        for span in range(4, 8):
+            quantise(tenth, passes_of(span))
+        overlap_passes(tenth, 4)
+
+        for span in range(0, SPANS, 2):
+            turn_in_drain(last, span)
+            turn_in_drain(last, span + 1)
+            empty(last, span, by_vector=False)
+            empty(last, span + 1, by_vector=True)
+            if span == 2:
+                overlap_passes(tenth, 5, count=3)
+            if span == 6:
+                square_overlap(tenth)
+            if span >= 4:
+                overlap_passes(last, span - 4, count=2, half=0)
+            quantise(last, passes_of(span))
+            quantise(last, passes_of(span + 1))
+        for half in range(2):
+            group_fidelity(0, half)
+        for half in range(2):
+            quantise_fidelity(0, half)
+        overlap_passes(last, 4, count=2, half=0)
+        overlap_passes(last, 0, count=4, half=1)
+        overlap_passes(last, 6, count=2, half=0)
+        overlap_passes(last, 4, count=4, half=1)
+        for half in range(2):
+            square_overlap(last, half)
+        for half in range(2):
+            group_fidelity(1, half)
+            quantise_fidelity(1, half)
+        for half in range(2):
+            project(half)

@@ -70,7 +70,7 @@ def tile_quantumkernelpca_kernel(tc, x, x_ref, mean_, components__words, compone
         ctx.enter_context(tc.manual_schedule())
 
         mean_rows = const.tile([P, RUN], BF16)
-        nc.gpsimd.memset(mean_rows[:].bitcast(I32), 0)
+        nc.vector.memset(mean_rows[:].bitcast(I32), 0)
         nc.scalar.dma_start(
             out=mean_rows[0 : SPANS * PACK, :], in_=mean_.rearrange("(s t i) -> (s t) i", t=PACK, i=RUN)
         )
@@ -379,45 +379,45 @@ def tile_quantumkernelpca_kernel(tc, x, x_ref, mean_, components__words, compone
                 square_overlap(coded_group)
         load_weight()
 
-        ninth, tenth, last = GROUPS - 3, GROUPS - 2, GROUPS - 1
+        before, middle, last = GROUPS - 3, GROUPS - 2, GROUPS - 1
         first, third = SLABS * last, SLABS * last + 2
         add_epsilon(first)
-        invert_norms(first)
         for span in range(3):
-            turn(tenth, span)
-        quantise(ninth, passes_of(6, QUARTER_SPANS))
-        quantise(ninth, passes_of(4, QUARTER_SPANS))
+            turn(middle, span)
+        quantise(before, passes_of(6, QUARTER_SPANS))
+        invert_norms(first)
+        quantise(before, passes_of(4, QUARTER_SPANS))
         scale_on_gpsimd(first)
-        overlap_passes(ninth, 4, count=2)
+        overlap_passes(before, 4, count=2)
         sum_squares(third + 1)
         for span in range(3):
-            empty(tenth, span, by_vector=True)
+            empty(middle, span, by_vector=True)
         for span in range(3):
-            quantise(tenth, passes_of(span))
+            quantise(middle, passes_of(span))
         scale_on_vector(first + 1)
-        turn(tenth, 3)
-        turn_in_drain(tenth, 4)
-        turn_in_drain(tenth, 5)
-        empty(tenth, 3, by_vector=False)
+        turn(middle, 3)
+        turn_in_drain(middle, 4)
+        turn_in_drain(middle, 5)
+        empty(middle, 3, by_vector=False)
         take_norms(third)
-        overlap_passes(ninth, 6, count=2)
-        empty(tenth, 4, by_vector=False)
+        overlap_passes(before, 6, count=2)
+        empty(middle, 4, by_vector=False)
         add_epsilon(third)
-        quantise(tenth, passes_of(3))
-        empty(tenth, 5, by_vector=False)
+        quantise(middle, passes_of(3))
+        empty(middle, 5, by_vector=False)
         invert_norms(third)
-        square_overlap(ninth)
+        square_overlap(before)
         scale_on_vector(third)
-        overlap_passes(tenth, 0, count=3)
-        turn_in_drain(tenth, 6)
-        turn_in_drain(tenth, 7)
-        overlap_passes(tenth, 3)
-        empty(tenth, 6, by_vector=False)
-        empty(tenth, 7, by_vector=False)
+        overlap_passes(middle, 0, count=3)
+        turn_in_drain(middle, 6)
+        turn_in_drain(middle, 7)
+        overlap_passes(middle, 3)
+        empty(middle, 6, by_vector=False)
+        empty(middle, 7, by_vector=False)
         scale_on_vector(third + 1)
         for span in range(4, 8):
-            quantise(tenth, passes_of(span))
-        overlap_passes(tenth, 4)
+            quantise(middle, passes_of(span))
+        overlap_passes(middle, 4)
 
         for span in range(0, SPANS, 2):
             turn_in_drain(last, span)
@@ -425,9 +425,9 @@ def tile_quantumkernelpca_kernel(tc, x, x_ref, mean_, components__words, compone
             empty(last, span, by_vector=False)
             empty(last, span + 1, by_vector=True)
             if span == 2:
-                overlap_passes(tenth, 5, count=3)
+                overlap_passes(middle, 5, count=3)
             if span == 6:
-                square_overlap(tenth)
+                square_overlap(middle)
             if span >= 4:
                 overlap_passes(last, span - 4, count=2, half=0)
             quantise(last, passes_of(span))

from contextlib import ExitStack

import concourse.mybir as mybir
from concourse.masks import make_identity

BF16 = mybir.dt.bfloat16
F32 = mybir.dt.float32
I32 = mybir.dt.int32
U32 = mybir.dt.uint32
U8 = mybir.dt.uint8
FP8X4 = mybir.dt.float8_e4m3fn_x4
ALU = mybir.AluOpType
ACT = mybir.ActivationFunctionType
AXIS = mybir.AxisListType

N_X = 512
N_REF = 1024
FEATURES = 8192
COMPONENTS = 128
EPS = 1e-8

P = 128
PACK = 4
K_PASS = P * PACK
PASSES = FEATURES // K_PASS
REF_PASSES = N_REF // K_PASS
SLAB_ROWS = P // PACK
SLAB_COLS = FEATURES // PACK
SLABS = P // SLAB_ROWS
BANK_BF16 = 1024
BANK_F32 = 512
RUN = 256
PAIR = 2
SPANS = SLAB_COLS // RUN
SPAN_PASSES = PASSES // SPANS
HALF_SPANS = SPANS // 2
QUARTER_SPANS = 2
QUARTER_PASSES = QUARTER_SPANS * SPAN_PASSES
GROUPS = (N_X + N_REF) // P
X_GROUPS = N_X // P
HALF = N_X // 2
SLAB_COUNT = GROUPS * SLABS
TOGETHER = 2
LOAD_AHEAD = 6
MEAN_TAGS = ("mean_lo", "mean_hi")
DRAIN_BANKS = 5
RELIEVED_GROUPS = (X_GROUPS + 1, X_GROUPS + 3)

FLOPS = 2 * N_X * N_REF * FEATURES + 2 * N_X * N_REF * COMPONENTS


def tile_quantumkernelpca_kernel(tc, x, x_ref, mean_, components__words, components__scales, out):
    nc = tc.nc
    with ExitStack() as ctx:
        const = ctx.enter_context(tc.tile_pool(name="const", bufs=1))
        raw_pool = ctx.enter_context(tc.tile_pool(name="raw", bufs=8))
        diff_pool = ctx.enter_context(tc.tile_pool(name="diff", bufs=8))
        unit_pool = ctx.enter_context(tc.tile_pool(name="unit", bufs=8))
        scratch = ctx.enter_context(tc.tile_pool(name="scratch", bufs=1))
        stats = ctx.enter_context(tc.tile_pool(name="stats", bufs=3))
        inv_pool = ctx.enter_context(tc.tile_pool(name="inv", bufs=8))
        grouped_pool = ctx.enter_context(tc.tile_pool(name="grouped", bufs=4))
        ref_pool = ctx.enter_context(tc.tile_pool(name="ref", bufs=2))
        fid_pool = ctx.enter_context(tc.tile_pool(name="fid", bufs=2))
        result_pool = ctx.enter_context(tc.tile_pool(name="result", bufs=2))
        psum_mean = ctx.enter_context(tc.psum_pool(name="psum_mean", bufs=1))
        psum_turn = ctx.enter_context(tc.psum_pool(name="psum_turn", bufs=3))
        psum_ov = ctx.enter_context(tc.psum_pool(name="psum_ov", bufs=2))
        psum_small = ctx.enter_context(tc.psum_pool(name="psum_small", bufs=1))
        ctx.enter_context(tc.manual_schedule())

        mean_rows = const.tile([P, RUN], BF16)
        nc.vector.memset(mean_rows[:].bitcast(I32), 0)
        nc.scalar.dma_start(
            out=mean_rows[0 : SPANS * PACK, :], in_=mean_.rearrange("(s t i) -> (s t) i", t=PACK, i=RUN)
        )
        ident = const.tile([P, P], F32)
        make_identity(nc, ident[:])
        pick = const.tile([P, SPANS, SLAB_ROWS, PACK], BF16)
        nc.vector.tensor_copy(
            out=pick[:],
            in_=ident[:, 0 : SPANS * PACK]
            .rearrange("p (s t) -> p s t", t=PACK)
            .unsqueeze(2)
            .to_broadcast([P, SPANS, SLAB_ROWS, PACK]),
        )
        picks = pick[:].rearrange("p s r t -> p (s r t)")

        mean_lo = psum_mean.tile([P, BANK_BF16], BF16, tag=MEAN_TAGS[0])
        mean_hi = psum_mean.tile([P, BANK_BF16], BF16, tag=MEAN_TAGS[1])
        mean_banks = [mean_lo, mean_hi]
        for s in range(SPANS):
            h, j = divmod(s, SPANS // 2)
            nc.tensor.matmul(
                out=mean_banks[h][:, RUN * j : RUN * (j + 1)],
                lhsT=picks[:, P * s : P * (s + 1)],
                rhs=mean_rows[:],
                start=True,
                stop=True,
            )

        warm = const.tile([P, 1], F32)
        nc.vector.memset(warm[:], 1.0)
        nc.scalar.activation(out=warm[:], in_=warm[:], func=ACT.Sqrt)
        row_of = const.tile([P, SLAB_ROWS], F32)
        nc.vector.tensor_reduce(
            out=row_of[:], in_=ident[:].rearrange("p (r t) -> p r t", t=PACK), axis=AXIS.X, op=ALU.add
        )
        same_row = const.tile([P, SLAB_ROWS, PACK], F32)

        w_words = const.tile([P, REF_PASSES, COMPONENTS], U32, align_bytes=64)
        w_scales = const.tile([P, REF_PASSES, COMPONENTS], U8, align_bytes=64)
        nc.vector.memset(w_scales[:].rearrange("p h n -> p (h n)").bitcast(I32), 0)
        nc.vector.tensor_copy(out=same_row[:], in_=row_of[:].unsqueeze(2).to_broadcast([P, SLAB_ROWS, PACK]))
        x_codes = const.tile([P, PASSES, N_X], U32, align_bytes=64)
        x_scales = const.tile([P, PASSES, N_X], U8, align_bytes=64)
        fid_codes = const.tile([P, REF_PASSES, N_X], U32, align_bytes=64)
        fid_scales = const.tile([P, REF_PASSES, N_X], U8, align_bytes=64)

        x_groups = x.rearrange("(c q) (s t i) -> c t q s i", q=P, t=PACK, i=RUN)
        ref_groups = x_ref.rearrange("(h q u) (s t i) -> h u t q s i", q=P, u=PACK, t=PACK, i=RUN)
        rows_of = [x_groups[c] for c in range(X_GROUPS)]
        rows_of += [ref_groups[h, u] for h in range(REF_PASSES) for u in range(PACK)]

        raws, diffs, sumsqs, norms, invs, units = {}, {}, {}, {}, {}, {}
        turneds, groupeds, codes_of, scales_of = {}, {}, {}, {}
        overlaps, fids, fid_groupeds = {}, {}, {}
        drained = []

        def load(k):
            if k >= SLAB_COUNT:
                return
            n, a = divmod(k, SLABS)
            raw = raw_pool.tile([P, SLAB_COLS], BF16)
            for spans in [range(0, SPANS // 2), range(SPANS // 2, SPANS)] if k == 0 else [range(SPANS)]:
                for t in range(PACK):
                    nc.sync.dma_start(
                        out=raw[t:P:PACK, RUN * spans.start : RUN * spans.stop].rearrange("r (s i) -> r s i", i=RUN),
                        in_=rows_of[n][t, SLAB_ROWS * a : SLAB_ROWS * (a + 1), spans.start : spans.stop],
                    )
            raws[k] = raw

        def subtract_mean(k):
            diff = diff_pool.tile([P, SLAB_COLS], F32)
            for h in range(2):
                cols = slice(BANK_BF16 * h, BANK_BF16 * (h + 1))
                nc.vector.tensor_tensor(out=diff[:, cols], in0=raws[k][:, cols], in1=mean_banks[h][:], op=ALU.subtract)
            diffs[k] = diff

        def sum_squares(k):
            n, a = divmod(k, SLABS)
            if a == 0:
                sumsq = stats.tile([P, SLABS], F32)
                sumsqs[n] = sumsq
            squares = scratch.tile([P, SLAB_COLS], BF16)
            nc.scalar.activation(out=squares[:], in_=diffs[k][:], func=ACT.Square, accum_out=sumsqs[n][:, a : a + 1])

        def take_norms(k):
            n, a = divmod(k, SLABS)
            row_sumsq = psum_small.tile([P, TOGETHER], F32, tag="small")
            nc.tensor.matmul(
                out=row_sumsq[:],
                lhsT=same_row[:].rearrange("p r t -> p (r t)"),
                rhs=sumsqs[n][:, a : a + TOGETHER],
                start=True,
                stop=True,
            )
            norm = stats.tile([P, TOGETHER], F32)
            nc.scalar.activation(out=norm[:], in_=row_sumsq[:], func=ACT.Sqrt)
            norms[k] = norm

        def add_epsilon(k):
            nc.vector.tensor_scalar_add(out=norms[k][:], in0=norms[k][:], scalar1=EPS)

        def invert_norms(k):
            inv = inv_pool.tile([P, TOGETHER], F32)
            nc.vector.reciprocal(out=inv[:], in_=norms[k][:])
            for i in range(TOGETHER):
                invs[k + i] = inv[:, i : i + 1]

        def scale_on_gpsimd(k):
            unit = unit_pool.tile([P, SLAB_COLS], BF16)
            nc.gpsimd.tensor_scalar(
                out=unit[:], in0=diffs[k][:], scalar1=invs[k], scalar2=0.0, op0=ALU.mult, op1=ALU.add
            )
            units[k] = unit

        def scale_on_vector(k):
            unit = unit_pool.tile([P, SLAB_COLS], BF16)
            nc.vector.tensor_scalar_mul(out=unit[:], in0=diffs[k][:], scalar1=invs[k])
            units[k] = unit

        def turn_into(turned, n, span):
            for a in range(SLABS):
                words = units[SLABS * n + a][:].bitcast(F32)
                nc.tensor.transpose(turned[:, P * a : P * (a + 1)], words[:, P * span : P * (span + 1)], ident[:])
            turneds[n, span] = turned

        def turn(n, span):
            turned = psum_turn.tile([P, BANK_F32], F32)
            turn_into(turned, n, span)

        def turn_in_drain(n, span):
            drained.append((n, span))
            place = len(drained) % DRAIN_BANKS
            if place < len(MEAN_TAGS):
                late_turned = psum_mean.tile([P, BANK_F32], F32, tag=MEAN_TAGS[place])
                turn_into(late_turned, n, span)
            else:
                turn(n, span)

        def empty(n, span, by_vector):
            quarter, b = divmod(span, QUARTER_SPANS)
            if (n, quarter) not in groupeds:
                grouped = grouped_pool.tile([P, QUARTER_PASSES, K_PASS], BF16, align_bytes=64)
                groupeds[n, quarter] = grouped
            passes = slice(SPAN_PASSES * b, SPAN_PASSES * (b + 1))
            words_out = groupeds[n, quarter][:, passes, :].bitcast(F32).rearrange("p w (q v) -> p w q v", v=PAIR)
            words_in = turneds[n, span][:].rearrange("p (q w v) -> p w q v", w=SPAN_PASSES, v=PAIR)
            if by_vector:
                nc.vector.tensor_copy(out=words_out, in_=words_in)
            else:
                nc.scalar.copy(out=words_out, in_=words_in)

        def quantise(n, passes):
            if n not in codes_of:
                if n < X_GROUPS:
                    cols = slice(P * n, P * (n + 1))
                    codes_of[n] = x_codes[:, :, cols]
                    scales_of[n] = x_scales[:, :, cols]
                else:
                    ref_codes = ref_pool.tile([P, PASSES, P], U32, align_bytes=64)
                    ref_scales = ref_pool.tile([P, PASSES, P], U8, align_bytes=64)
                    codes_of[n] = ref_codes[:]
                    scales_of[n] = ref_scales[:]
            width = 1 if n < X_GROUPS else len(passes)
            for g in passes if n < X_GROUPS else passes[:1]:
                quarter, i = divmod(g, QUARTER_PASSES)
                nc.vector.quantize_mx(
                    out=codes_of[n][:, g : g + width, :].rearrange("p g c -> p (g c)").bitcast(FP8X4),
                    scales=scales_of[n][:, g : g + width, :].rearrange("p g c -> p (g c)"),
                    in_=groupeds[n, quarter][:, i : i + width, :].rearrange("p w c -> p (w c)"),
                )

        def passes_of(span, count=1):
            return range(SPAN_PASSES * span, SPAN_PASSES * (span + count))

        def overlap_passes(n, span, count=1, half=None):
            if n < X_GROUPS:
                return
            cols = slice(0, N_X) if half is None else slice(half * HALF, (half + 1) * HALF)
            for g in passes_of(span, count):
                if g == 0:
                    overlap = psum_ov.tile([P, N_X], F32)
                    overlaps[n, half] = overlap
                nc.tensor.matmul_mx(
                    out=overlaps[n, half][:, 0 : cols.stop - cols.start],
                    lhsT=codes_of[n][:, g, :].bitcast(FP8X4),
                    lhsT_scale=scales_of[n][:, g, :],
                    rhs=x_codes[:, g, cols].bitcast(FP8X4),
                    rhs_scale=x_scales[:, g, cols],
                    start=(g == 0),
                    stop=(g == PASSES - 1),
                )

        def square_overlap(n, half=None):
            if n < X_GROUPS:
                return
            h, u = divmod(n - X_GROUPS, PACK)
            if u == 0:
                fid = fid_pool.tile([P, PACK, N_X], BF16)
                fids[h] = fid
            cols = slice(0, N_X) if half is None else slice(half * HALF, (half + 1) * HALF)
            nc.scalar.activation(
                out=fids[h][:, u, cols], in_=overlaps[n, half][:, 0 : cols.stop - cols.start], func=ACT.Square
            )

        def group_fidelity(h, half):
            cols = slice(half * HALF, (half + 1) * HALF)
            fid_grouped = fid_pool.tile([P, HALF, PACK], BF16, align_bytes=64)
            nc.vector.tensor_copy(
                out=fid_grouped[:].rearrange("p (c i) u -> p c u i", i=PACK),
                in_=fids[h][:, :, cols].rearrange("p u (c i) -> p c u i", i=PACK),
            )
            fid_groupeds[h, half] = fid_grouped

        def quantise_fidelity(h, half):
            cols = slice(half * HALF, (half + 1) * HALF)
            nc.vector.quantize_mx(
                out=fid_codes[:, h, cols].bitcast(FP8X4),
                scales=fid_scales[:, h, cols],
                in_=fid_groupeds[h, half][:].rearrange("p i u -> p (i u)"),
            )

        def load_weight():
            for h in range(REF_PASSES):
                nc.sync.dma_start(
                    out=w_words[:, h, :].bitcast(I32),
                    in_=components__words[h].rearrange("p n t -> p (n t)").bitcast(I32),
                )
                for quad in range(4):
                    nc.sync.dma_start(
                        out=w_scales[32 * quad : 32 * quad + 4, h, :].bitcast(I32),
                        in_=components__scales[h, 4 * quad : 4 * quad + 4, :].bitcast(I32),
                    )

        def project(half):
            blocks = HALF // P
            projected = psum_small.tile([P, blocks, COMPONENTS], F32, tag="small")
            for i in range(blocks):
                block = blocks * half + i
                cols = slice(P * block, P * (block + 1))
                for h in range(REF_PASSES):
                    nc.tensor.matmul_mx(
                        out=projected[:, i, :],
                        lhsT=fid_codes[:, h, cols].bitcast(FP8X4),
                        lhsT_scale=fid_scales[:, h, cols],
                        rhs=w_words[:, h, :].bitcast(FP8X4),
                        rhs_scale=w_scales[:, h, :],
                        start=(h == 0),
                        stop=(h == REF_PASSES - 1),
                    )
            result = result_pool.tile([P, blocks, COMPONENTS], F32)
            nc.vector.tensor_copy(out=result[:], in_=projected[:])
            nc.sync.dma_start(
                out=out.rearrange("(c p) n -> p c n", p=P)[:, blocks * half : blocks * (half + 1), :], in_=result[:]
            )

        for k in range(LOAD_AHEAD):
            load(k)
        for k in range(0, SLAB_COUNT, TOGETHER):
            scaled = k - 4
            turned_group, turned_half = divmod(k // TOGETHER - 4, 2)
            coded_group, coded_half = divmod(k // TOGETHER - 5, 2)
            t0 = HALF_SPANS * turned_half
            c0 = HALF_SPANS * coded_half

            if scaled >= 0:
                add_epsilon(scaled)
            load(k + LOAD_AHEAD)
            if turned_group >= 0:
                for span in range(t0, t0 + 3):
                    turn(turned_group, span)
            if coded_group >= 0:
                last_call = 1 if coded_group < X_GROUPS else QUARTER_PASSES
                early = passes_of(c0, QUARTER_SPANS)
                quantise(coded_group, passes_of(c0 + QUARTER_SPANS, QUARTER_SPANS))
                quantise(coded_group, range(early.start, early.stop - last_call))
            if scaled >= 0:
                invert_norms(scaled)
            if coded_group >= 0:
                quantise(coded_group, range(early.stop - last_call, early.stop))
            if scaled >= 0:
                scale_on_gpsimd(scaled)
                scale_on_gpsimd(scaled + 1)
            if turned_group >= 0:
                empty(turned_group, t0, by_vector=True)
            if k > 0:
                sum_squares(k - 1)
            subtract_mean(k)
            if turned_group >= 0:
                empty(turned_group, t0 + 1, by_vector=False)
            if coded_group >= 0:
                overlap_passes(coded_group, c0)
            if turned_group >= 0:
                empty(turned_group, t0 + 2, by_vector=False)
                turn(turned_group, t0 + 3)
                empty(turned_group, t0 + 3, by_vector=turned_group in RELIEVED_GROUPS and turned_half == 1)
            if k >= 2:
                take_norms(k - 2)
            if coded_group >= 0:
                overlap_passes(coded_group, c0 + 1)
            load(k + 1 + LOAD_AHEAD)
            if coded_group >= 0:
                overlap_passes(coded_group, c0 + 2, count=2)
            sum_squares(k)
            subtract_mean(k + 1)
            if coded_group >= 0 and coded_half == 1:
                square_overlap(coded_group)
        load_weight()

        before, middle, last = GROUPS - 3, GROUPS - 2, GROUPS - 1
        first, third = SLABS * last, SLABS * last + 2
        add_epsilon(first)
        for span in range(3):
            turn(middle, span)
        quantise(before, passes_of(6, QUARTER_SPANS))
        invert_norms(first)
        quantise(before, passes_of(4, QUARTER_SPANS))
        scale_on_gpsimd(first)
        overlap_passes(before, 4, count=2)
        sum_squares(third + 1)
        for span in range(3):
            empty(middle, span, by_vector=True)
        for span in range(3):
            quantise(middle, passes_of(span))
        scale_on_vector(first + 1)
        turn(middle, 3)
        turn_in_drain(middle, 4)
        turn_in_drain(middle, 5)
        empty(middle, 3, by_vector=False)
        take_norms(third)
        overlap_passes(before, 6, count=2)
        empty(middle, 4, by_vector=False)
        add_epsilon(third)
        quantise(middle, passes_of(3))
        empty(middle, 5, by_vector=False)
        invert_norms(third)
        square_overlap(before)
        scale_on_vector(third)
        overlap_passes(middle, 0, count=3)
        turn_in_drain(middle, 6)
        turn_in_drain(middle, 7)
        overlap_passes(middle, 3)
        empty(middle, 6, by_vector=False)
        empty(middle, 7, by_vector=False)
        scale_on_vector(third + 1)
        for span in range(4, 8):
            quantise(middle, passes_of(span))
        overlap_passes(middle, 4)

        for span in range(0, SPANS, 2):
            turn_in_drain(last, span)
            turn_in_drain(last, span + 1)
            empty(last, span, by_vector=False)
            empty(last, span + 1, by_vector=True)
            if span == 2:
                overlap_passes(middle, 5, count=3)
            if span == 6:
                square_overlap(middle)
            if span >= 4:
                overlap_passes(last, span - 4, count=2, half=0)
            quantise(last, passes_of(span))
            quantise(last, passes_of(span + 1))
        for half in range(2):
            group_fidelity(0, half)
        for half in range(2):
            quantise_fidelity(0, half)
        overlap_passes(last, 4, count=2, half=0)
        overlap_passes(last, 0, count=4, half=1)
        overlap_passes(last, 6, count=2, half=0)
        overlap_passes(last, 4, count=4, half=1)
        for half in range(2):
            square_overlap(last, half)
        for half in range(2):
            group_fidelity(1, half)
            quantise_fidelity(1, half)
        for half in range(2):
            project(half)
